import numpy as np
import ml_dtypes


def mxq(x, axis, fmt="e4m3"):
    dtype, down = {"e4m3": (ml_dtypes.float8_e4m3fn, 7), "e5m2": (ml_dtypes.float8_e5m2, 14)}[fmt]
    v = np.moveaxis(np.asarray(x, np.float32).astype(ml_dtypes.bfloat16).astype(np.float64), axis, -1)
    blocks = v.reshape(v.shape[:-1] + (-1, 32))
    amax = np.abs(blocks).max(-1, keepdims=True)
    byte = np.maximum(np.where(amax > 0, np.frexp(amax)[1] - 1 + 127, 0) - down, 1)
    scale = np.exp2(byte - 127.0)
    codes = (blocks / scale).astype(np.float32).astype(dtype).astype(np.float64)
    return np.moveaxis((codes * scale).reshape(v.shape), -1, axis)


WIDE = False


def mx_kscale(k):
    if not WIDE:
        return np.ones(k)
    levels = np.array([10, -10, 5, -5, 0])
    a = np.random.permutation(np.resize(levels, k // 512 * 4)).reshape(k // 512, 4)
    idx = np.arange(k)
    return np.exp2(a[idx // 512, idx % 128 // 32])


BF16 = ml_dtypes.bfloat16


def bf(x):
    return np.asarray(x, np.float32).astype(BF16)


def f64(x):
    return np.asarray(x).astype(np.float64)


B, S, H, DH, C = 2, 1024, 2048, 256, 512
SCALE_BASE = 2.0 ** 9


def rotate_every_two(y):
    y1 = y[..., ::2]
    y2 = y[..., 1::2]
    return np.stack((-y2, y1), axis=-1).reshape(y.shape)


def xpos(y, downscale):
    L, D = y.shape[-2], y.shape[-1]
    d = D // 2
    scale_vec = (np.arange(0, D, 2) + 0.4 * D) / (1.4 * D)
    min_pos = (-L) // 2
    power = np.arange(min_pos, L + min_pos) / SCALE_BASE
    scale = scale_vec ** power[:, None]
    inv_freq = 1.0 / (10000.0 ** (np.arange(d) / d))
    sinusoid = np.arange(L)[:, None] * inv_freq
    sin, cos = np.sin(sinusoid), np.cos(sinusoid)
    if downscale:
        scale = 1.0 / scale
    sin = np.repeat(sin * scale, 2, axis=-1)
    cos = np.repeat(cos * scale, 2, axis=-1)
    return y * cos + rotate_every_two(y) * sin


def setup_inputs():
    s = mx_kscale(H)
    return {"x": bf(np.random.standard_normal((B, S, H)) * s),
            "w_q": bf(np.random.standard_normal((H, DH)) * 0.5 / np.sqrt(H) / s[:, None]),
            "w_k": bf(np.random.standard_normal((H, DH)) * 0.5 / np.sqrt(H) / s[:, None]),
            "w_v": bf(np.random.standard_normal((H, DH)) * 0.25 / np.sqrt(H) / s[:, None])}


def reference(x, w_q, w_k, w_v):
    xq = mxq(f64(x), 2, "e4m3")
    q = xpos(xq @ mxq(f64(w_q), 0, "e4m3"), False)
    k = xpos(xq @ mxq(f64(w_k), 0, "e4m3"), True)
    v = xq @ mxq(f64(w_v), 0, "e4m3")
    return q, k, v

@@ -1,0 +1,282 @@
+from contextlib import ExitStack
+import math
+
+import concourse.mybir as mybir
+from concourse.masks import make_identity
+
+F32 = mybir.dt.float32
+BF16 = mybir.dt.bfloat16
+I32 = mybir.dt.int32
+U32 = mybir.dt.uint32
+U8 = mybir.dt.uint8
+FP8X4 = mybir.dt.float8_e4m3fn_x4
+ALU = mybir.AluOpType
+ACT = mybir.ActivationFunctionType
+
+P = 128
+BATCH, SEQ, HID, DH = 2, 1024, 2048, 256
+PAIRS = DH // 2
+TILES = SEQ // P
+PACK = 4
+PASSES = HID // (P * PACK)
+WORDS = HID // 2
+ROUND = 2
+ROUNDS = BATCH * TILES // ROUND
+AHEAD = 5
+
+ROTARY_BASE = 10000.0
+SCALE_BASE = 512.0
+ROUND_MAGIC = 1.5 * 2.0**23
+
+FLOPS = 2 * BATCH * SEQ * HID * 3 * DH
+
+
+def tile_retblock_pa_kernel(tc, x, w_q, w_k, w_v, out_0, out_1, out_2):
+    nc = tc.nc
+    with ExitStack() as ctx:
+        const = ctx.enter_context(tc.tile_pool(name="const", bufs=1))
+        x_raw_pool = ctx.enter_context(tc.tile_pool(name="x_raw_pool", bufs=AHEAD))
+        x_mx_pool = ctx.enter_context(tc.tile_pool(name="x_mx_pool", bufs=3))
+        w_grouped_pool = ctx.enter_context(tc.tile_pool(name="w_grouped_pool", bufs=2))
+        work = ctx.enter_context(tc.tile_pool(name="work", bufs=3))
+        xt_psum = ctx.enter_context(tc.psum_pool(name="xt_psum", bufs=4))
+        qk_psum = ctx.enter_context(tc.psum_pool(name="qk_psum", bufs=3))
+        v_psum = ctx.enter_context(tc.psum_pool(name="v_psum", bufs=1))
+
+        def batch_of(r):
+            return r % BATCH
+
+        def first_tile_of(r):
+            return (r // BATCH) * ROUND
+
+        def load_x(r):
+            x_raw = x_raw_pool.tile([P, ROUND * HID], BF16, name="x_raw")
+            rows = x[batch_of(r)].rearrange("(p t) k -> p (t k)", t=TILES)
+            first = first_tile_of(r) * HID
+            nc.sync.dma_start(out=x_raw[:], in_=rows[:, first : first + ROUND * HID])
+            return x_raw
+
+        def load_w(w, name):
+            w_raw = const.tile([P, PASSES * PACK, DH], BF16, name=name)
+            nc.sync.dma_start(
+                out=w_raw[:].rearrange("p (a e) c -> p a (e c)", e=2),
+                in_=w.rearrange("(a p e) c -> p a (e c)", p=P, e=2),
+            )
+            return w_raw
+
+        def quantise_w(w_raw, name):
+            w_grouped = w_grouped_pool.tile(
+                [P, PASSES, DH, PACK], BF16, align_bytes=64, name="w_grouped"
+            )
+            for g in range(PASSES):
+                nc.vector.tensor_copy(
+                    out=w_grouped[:, g].rearrange("p (c i) t -> p c t i", i=4),
+                    in_=w_raw[:, g * PACK : (g + 1) * PACK, :].rearrange(
+                        "p t (c i) -> p c t i", i=4
+                    ),
+                )
+            codes = const.tile([P, PASSES * DH], U32, align_bytes=64, name=name + "_codes")
+            scales = const.tile([P, PASSES * DH], U8, align_bytes=64, name=name + "_scales")
+            nc.vector.quantize_mx(
+                out=codes[:].bitcast(FP8X4),
+                scales=scales[:],
+                in_=w_grouped[:].rearrange("p g c t -> p (g c t)"),
+            )
+            return codes, scales
+
+        def transpose_x(x_raw):
+            words = x_raw[:].bitcast(F32)
+            x_grouped = x_mx_pool.tile([P, ROUND * HID], BF16, align_bytes=64, name="x_grouped")
+            grouped_words = x_grouped[:].bitcast(F32)
+            for bank in range(ROUND * WORDS // (4 * P)):
+                xt = xt_psum.tile([P, 4, P], F32, name="xt")
+                for a in range(4):
+                    first = (bank * 4 + a) * P
+                    nc.tensor.transpose(xt[:, a, :], words[:, first : first + P], ident[:])
+                first = bank * 4 * P
+                nc.scalar.copy(
+                    out=grouped_words[:, first : first + 4 * P].rearrange(
+                        "p (g r u) -> p g r u", g=2, u=2
+                    ),
+                    in_=xt[:].rearrange("p (g u) r -> p g r u", u=2),
+                )
+            return x_grouped
+
+        def quantise_x(x_grouped):
+            codes = x_mx_pool.tile([P, ROUND * PASSES * P], U32, align_bytes=64, name="x_codes")
+            scales = x_mx_pool.tile([P, ROUND * PASSES * P], U8, align_bytes=64, name="x_scales")
+            for i in range(ROUND):
+                cols = slice(i * PASSES * P, (i + 1) * PASSES * P)
+                nc.vector.quantize_mx(
+                    out=codes[:, cols].bitcast(FP8X4),
+                    scales=scales[:, cols],
+                    in_=x_grouped[:, i * HID : (i + 1) * HID],
+                )
+            return codes, scales
+
+        def project(out, x_mx, i, w_mx):
+            x_codes, x_scales = x_mx
+            w_codes, w_scales = w_mx
+            for g in range(PASSES):
+                tokens = slice((i * PASSES + g) * P, (i * PASSES + g + 1) * P)
+                features = slice(g * DH, (g + 1) * DH)
+                nc.tensor.matmul_mx(
+                    out=out,
+                    lhsT=x_codes[:, tokens].bitcast(FP8X4),
+                    lhsT_scale=x_scales[:, tokens],
+                    rhs=w_codes[:, features].bitcast(FP8X4),
+                    rhs_scale=w_scales[:, features],
+                    start=(g == 0),
+                    stop=(g == PASSES - 1),
+                )
+
+        def build_tables():
+            j_int = const.tile([P, PAIRS], I32, name="j_int")
+            nc.gpsimd.iota(j_int[:], pattern=[[1, PAIRS]], base=0, channel_multiplier=0)
+            pos_int = const.tile([P, TILES], I32, name="pos_int")
+            nc.gpsimd.iota(pos_int[:], pattern=[[1, TILES]], base=0, channel_multiplier=TILES)
+            base = const.tile([P, PAIRS], F32, name="base")
+            nc.vector.tensor_copy(out=base[:], in_=j_int[:])
+            pos = const.tile([P, TILES], F32, name="pos")
+            nc.vector.tensor_copy(out=pos[:], in_=pos_int[:])
+
+            nc.vector.tensor_scalar(
+                out=base[:], in0=base[:], scalar1=2.0 / (1.4 * DH), scalar2=0.4 / 1.4,
+                op0=ALU.mult, op1=ALU.add,
+            )
+            nc.scalar.activation(out=base[:], in_=base[:], func=ACT.Ln)
+            centred = const.tile([P, TILES], F32, name="centred")
+            nc.vector.tensor_scalar(
+                out=centred[:], in0=pos[:], scalar1=float(SEQ // 2), scalar2=1.0 / SCALE_BASE,
+                op0=ALU.subtract, op1=ALU.mult,
+            )
+            plain = [P, TILES, PAIRS]
+            log_z = const.tile(plain, F32, name="log_z")
+            nc.vector.tensor_tensor(
+                out=log_z[:],
+                in0=centred[:].unsqueeze(2).to_broadcast(plain),
+                in1=base[:].unsqueeze(1).to_broadcast(plain),
+                op=ALU.mult,
+            )
+            both = [P, TILES, 2, PAIRS]
+            zoom = const.tile(both, F32, name="zoom")
+            nc.scalar.activation(out=zoom[:, :, 0, :], in_=log_z[:], func=ACT.Exp)
+            nc.scalar.activation(out=zoom[:, :, 1, :], in_=log_z[:], func=ACT.Exp, scale=-1.0)
+
+            freq = const.tile([P, PAIRS], F32, name="freq")
+            nc.vector.memset(freq[:, 0:1], 1.0)
+            for doubling in range(7):
+                width = 2**doubling
+                nc.vector.tensor_scalar(
+                    out=freq[:, width : 2 * width], in0=freq[:, 0:width],
+                    scalar1=ROTARY_BASE ** (-width / PAIRS), scalar2=None, op0=ALU.mult,
+                )
+            pos_turns = const.tile([P, TILES], F32, name="pos_turns")
+            nc.vector.tensor_scalar(
+                out=pos_turns[:], in0=pos[:], scalar1=1.0 / (2.0 * math.pi), scalar2=None,
+                op0=ALU.mult,
+            )
+            angle = const.tile(plain, F32, name="angle")
+            nc.vector.tensor_tensor(
+                out=angle[:],
+                in0=pos_turns[:].unsqueeze(2).to_broadcast(plain),
+                in1=freq[:].unsqueeze(1).to_broadcast(plain),
+                op=ALU.mult,
+            )
+            whole = const.tile(plain, F32, name="whole")
+            nc.vector.tensor_scalar(
+                out=whole[:], in0=angle[:], scalar1=ROUND_MAGIC, scalar2=ROUND_MAGIC,
+                op0=ALU.add, op1=ALU.subtract,
+            )
+            nc.vector.tensor_tensor(out=angle[:], in0=angle[:], in1=whole[:], op=ALU.subtract)
+            sine = const.tile(plain, F32, name="sine")
+            nc.scalar.activation(out=sine[:], in_=angle[:], func=ACT.Sin, scale=2.0 * math.pi)
+            cosine = const.tile(plain, F32, name="cosine")
+            nc.scalar.activation(out=cosine[:], in_=angle[:], func=ACT.Sin, scale=math.pi)
+            nc.scalar.activation(out=cosine[:], in_=cosine[:], func=ACT.Square)
+            nc.scalar.activation(out=cosine[:], in_=cosine[:], func=ACT.Copy, scale=-2.0, bias=1.0)
+
+            cos_tab = const.tile(both, F32, name="cos_tab")
+            nc.vector.tensor_tensor(
+                out=cos_tab[:], in0=cosine[:].unsqueeze(2).to_broadcast(both), in1=zoom[:],
+                op=ALU.mult,
+            )
+            sin_tab = const.tile(both, F32, name="sin_tab")
+            nc.vector.tensor_tensor(
+                out=sin_tab[:], in0=sine[:].unsqueeze(2).to_broadcast(both), in1=zoom[:],
+                op=ALU.mult,
+            )
+            return cos_tab, sin_tab
+
+        def rotate(qk, t, rotated):
+            y = qk[:].rearrange("p (mj e) -> p mj e", e=2)
+            cos_t = cos_tab[:, t].rearrange("p m j -> p (m j)")
+            sin_t = sin_tab[:, t].rearrange("p m j -> p (m j)")
+            straight = work.tile([P, 2 * PAIRS, 2], F32, name="straight")
+            nc.vector.tensor_tensor(
+                out=straight[:], in0=y, in1=cos_t.unsqueeze(2).to_broadcast([P, 2 * PAIRS, 2]),
+                op=ALU.mult,
+            )
+            crossed = work.tile([P, 2, 2 * PAIRS], F32, name="crossed")
+            nc.vector.scalar_tensor_tensor(
+                out=crossed[:, 0, :], in0=y[:, :, 1], scalar=-1.0, in1=sin_t,
+                op0=ALU.mult, op1=ALU.mult,
+            )
+            nc.vector.tensor_tensor(out=crossed[:, 1, :], in0=y[:, :, 0], in1=sin_t, op=ALU.mult)
+            nc.vector.tensor_tensor(
+                out=rotated.rearrange("p m (j e) -> p m j e", e=2),
+                in0=straight[:].rearrange("p (m j) e -> p m j e", m=2),
+                in1=crossed[:].rearrange("p e (m j) -> p m j e", m=2),
+                op=ALU.add,
+            )
+
+        def store(out, r, tile_rows):
+            rows = out[batch_of(r)].rearrange("(p t) d -> p (t d)", t=TILES)
+            first = first_tile_of(r) * DH
+            nc.sync.dma_start(out=rows[:, first : first + ROUND * DH], in_=tile_rows)
+
+        ident = const.tile([P, P], F32, name="ident")
+        make_identity(nc, ident[:])
+
+        x_raw = {}
+        x_raw[0] = load_x(0)
+        w_raw = [load_w(w_q, "wq_raw"), load_w(w_k, "wk_raw"), load_w(w_v, "wv_raw")]
+        for r in range(1, AHEAD):
+            x_raw[r] = load_x(r)
+
+        cos_tab, sin_tab = build_tables()
+
+        x_mx = {}
+        x_grouped = transpose_x(x_raw[0])
+        w_mx = [quantise_w(w_raw[0], "wq")]
+        x_mx[0] = quantise_x(x_grouped)
+        w_mx.append(quantise_w(w_raw[1], "wk"))
+        w_mx.append(quantise_w(w_raw[2], "wv"))
+
+        for r in range(ROUNDS):
+            if r + 1 < ROUNDS:
+                x_grouped = transpose_x(x_raw[r + 1])
+            if r + AHEAD < ROUNDS:
+                x_raw[r + AHEAD] = load_x(r + AHEAD)
+
+            qk_banks = []
+            v_bank = v_psum.tile([P, ROUND, DH], F32, name="v_bank")
+            for i in range(ROUND):
+                qk = qk_psum.tile([P, 2 * DH], F32, name="qk")
+                project(qk[:, 0:DH], x_mx[r], i, w_mx[0])
+                project(qk[:, DH : 2 * DH], x_mx[r], i, w_mx[1])
+                project(v_bank[:, i, :], x_mx[r], i, w_mx[2])
+                qk_banks.append(qk)
+
+            if r + 1 < ROUNDS:
+                x_mx[r + 1] = quantise_x(x_grouped)
+
+            rotated = work.tile([P, 2, ROUND, DH], F32, name="rotated")
+            for i in range(ROUND):
+                rotate(qk_banks[i], first_tile_of(r) + i, rotated[:, :, i, :])
+            v_rows = work.tile([P, ROUND * DH], F32, name="v_rows")
+            nc.scalar.copy(out=v_rows[:], in_=v_bank[:].rearrange("p i d -> p (i d)"))
+
+            store(out_2, r, v_rows[:])
+            store(out_0, r, rotated[:, 0].rearrange("p i d -> p (i d)"))
+            store(out_1, r, rotated[:, 1].rearrange("p i d -> p (i d)"))

@@ -42,6 +42,7 @@ def tile_retblock_pa_kernel(tc, x, w_q, w_k, w_v, out_0, out_1, out_2):
         xt_psum = ctx.enter_context(tc.psum_pool(name="xt_psum", bufs=4))
         qk_psum = ctx.enter_context(tc.psum_pool(name="qk_psum", bufs=3))
         v_psum = ctx.enter_context(tc.psum_pool(name="v_psum", bufs=1))
+        ctx.enter_context(tc.manual_schedule())
 
         def batch_of(r):
             return r % BATCH
@@ -64,7 +65,7 @@ def tile_retblock_pa_kernel(tc, x, w_q, w_k, w_v, out_0, out_1, out_2):
             )
             return w_raw
 
-        def quantise_w(w_raw, name):
+        def regroup_w(w_raw):
             w_grouped = w_grouped_pool.tile(
                 [P, PASSES, DH, PACK], BF16, align_bytes=64, name="w_grouped"
             )
@@ -75,6 +76,9 @@ def tile_retblock_pa_kernel(tc, x, w_q, w_k, w_v, out_0, out_1, out_2):
                         "p t (c i) -> p c t i", i=4
                     ),
                 )
+            return w_grouped
+
+        def quantise_w(w_grouped, name):
             codes = const.tile([P, PASSES * DH], U32, align_bytes=64, name=name + "_codes")
             scales = const.tile([P, PASSES * DH], U8, align_bytes=64, name=name + "_scales")
             nc.vector.quantize_mx(
@@ -130,39 +134,39 @@ def tile_retblock_pa_kernel(tc, x, w_q, w_k, w_v, out_0, out_1, out_2):
                     stop=(g == PASSES - 1),
                 )
 
-        def build_tables():
+        plain = [P, TILES, PAIRS]
+        both = [P, TILES, 2, PAIRS]
+        angle = const.tile(plain, F32, name="angle")
+        zoom = const.tile(both, F32, name="zoom")
+        sine = const.tile(plain, F32, name="sine")
+        cosine = const.tile(plain, F32, name="cosine")
+        cos_tab = const.tile(both, F32, name="cos_tab")
+        sin_tab = const.tile(both, F32, name="sin_tab")
+
+        def table_columns():
             j_int = const.tile([P, PAIRS], I32, name="j_int")
             nc.gpsimd.iota(j_int[:], pattern=[[1, PAIRS]], base=0, channel_multiplier=0)
             pos_int = const.tile([P, TILES], I32, name="pos_int")
             nc.gpsimd.iota(pos_int[:], pattern=[[1, TILES]], base=0, channel_multiplier=TILES)
-            base = const.tile([P, PAIRS], F32, name="base")
-            nc.vector.tensor_copy(out=base[:], in_=j_int[:])
-            pos = const.tile([P, TILES], F32, name="pos")
-            nc.vector.tensor_copy(out=pos[:], in_=pos_int[:])
-
+            log_base = const.tile([P, PAIRS], F32, name="log_base")
+            nc.vector.tensor_copy(out=log_base[:], in_=j_int[:])
             nc.vector.tensor_scalar(
-                out=base[:], in0=base[:], scalar1=2.0 / (1.4 * DH), scalar2=0.4 / 1.4,
+                out=log_base[:], in0=log_base[:], scalar1=2.0 / (1.4 * DH), scalar2=0.4 / 1.4,
                 op0=ALU.mult, op1=ALU.add,
             )
-            nc.scalar.activation(out=base[:], in_=base[:], func=ACT.Ln)
+            nc.scalar.activation(out=log_base[:], in_=log_base[:], func=ACT.Ln)
+            pos = const.tile([P, TILES], F32, name="pos")
+            nc.vector.tensor_copy(out=pos[:], in_=pos_int[:])
             centred = const.tile([P, TILES], F32, name="centred")
             nc.vector.tensor_scalar(
                 out=centred[:], in0=pos[:], scalar1=float(SEQ // 2), scalar2=1.0 / SCALE_BASE,
                 op0=ALU.subtract, op1=ALU.mult,
             )
-            plain = [P, TILES, PAIRS]
-            log_z = const.tile(plain, F32, name="log_z")
-            nc.vector.tensor_tensor(
-                out=log_z[:],
-                in0=centred[:].unsqueeze(2).to_broadcast(plain),
-                in1=base[:].unsqueeze(1).to_broadcast(plain),
-                op=ALU.mult,
+            pos_turns = const.tile([P, TILES], F32, name="pos_turns")
+            nc.vector.tensor_scalar(
+                out=pos_turns[:], in0=pos[:], scalar1=1.0 / (2.0 * math.pi), scalar2=None,
+                op0=ALU.mult,
             )
-            both = [P, TILES, 2, PAIRS]
-            zoom = const.tile(both, F32, name="zoom")
-            nc.scalar.activation(out=zoom[:, :, 0, :], in_=log_z[:], func=ACT.Exp)
-            nc.scalar.activation(out=zoom[:, :, 1, :], in_=log_z[:], func=ACT.Exp, scale=-1.0)
-
             freq = const.tile([P, PAIRS], F32, name="freq")
             nc.vector.memset(freq[:, 0:1], 1.0)
             for doubling in range(7):
@@ -171,42 +175,55 @@ def tile_retblock_pa_kernel(tc, x, w_q, w_k, w_v, out_0, out_1, out_2):
                     out=freq[:, width : 2 * width], in0=freq[:, 0:width],
                     scalar1=ROTARY_BASE ** (-width / PAIRS), scalar2=None, op0=ALU.mult,
                 )
-            pos_turns = const.tile([P, TILES], F32, name="pos_turns")
-            nc.vector.tensor_scalar(
-                out=pos_turns[:], in0=pos[:], scalar1=1.0 / (2.0 * math.pi), scalar2=None,
-                op0=ALU.mult,
+            return log_base, centred, pos_turns, freq
+
+        def table_zoom(log_base, centred):
+            log_z = const.tile(plain, F32, name="log_z")
+            nc.gpsimd.tensor_tensor(
+                out=log_z[:],
+                in0=centred[:].unsqueeze(2).to_broadcast(plain),
+                in1=log_base[:].unsqueeze(1).to_broadcast(plain),
+                op=ALU.mult,
             )
-            angle = const.tile(plain, F32, name="angle")
-            nc.vector.tensor_tensor(
+            nc.scalar.activation(out=zoom[:, :, 0, :], in_=log_z[:], func=ACT.Exp)
+            nc.scalar.activation(out=zoom[:, :, 1, :], in_=log_z[:], func=ACT.Exp, scale=-1.0)
+
+        def table_turns(pos_turns, freq):
+            nc.gpsimd.tensor_tensor(
                 out=angle[:],
                 in0=pos_turns[:].unsqueeze(2).to_broadcast(plain),
                 in1=freq[:].unsqueeze(1).to_broadcast(plain),
                 op=ALU.mult,
             )
+
+        def table_fraction():
             whole = const.tile(plain, F32, name="whole")
             nc.vector.tensor_scalar(
                 out=whole[:], in0=angle[:], scalar1=ROUND_MAGIC, scalar2=ROUND_MAGIC,
                 op0=ALU.add, op1=ALU.subtract,
             )
-            nc.vector.tensor_tensor(out=angle[:], in0=angle[:], in1=whole[:], op=ALU.subtract)
-            sine = const.tile(plain, F32, name="sine")
-            nc.scalar.activation(out=sine[:], in_=angle[:], func=ACT.Sin, scale=2.0 * math.pi)
-            cosine = const.tile(plain, F32, name="cosine")
-            nc.scalar.activation(out=cosine[:], in_=angle[:], func=ACT.Sin, scale=math.pi)
-            nc.scalar.activation(out=cosine[:], in_=cosine[:], func=ACT.Square)
-            nc.scalar.activation(out=cosine[:], in_=cosine[:], func=ACT.Copy, scale=-2.0, bias=1.0)
+            nc.gpsimd.tensor_tensor(out=angle[:], in0=angle[:], in1=whole[:], op=ALU.subtract)
 
-            cos_tab = const.tile(both, F32, name="cos_tab")
-            nc.vector.tensor_tensor(
-                out=cos_tab[:], in0=cosine[:].unsqueeze(2).to_broadcast(both), in1=zoom[:],
-                op=ALU.mult,
+        def table_waves(first_tile):
+            t = slice(first_tile, first_tile + ROUND)
+            nc.scalar.activation(out=cosine[:, t], in_=angle[:, t], func=ACT.Sin, scale=math.pi)
+            nc.scalar.activation(out=sine[:, t], in_=angle[:, t], func=ACT.Sin, scale=2.0 * math.pi)
+            nc.scalar.activation(out=cosine[:, t], in_=cosine[:, t], func=ACT.Square)
+            nc.scalar.activation(
+                out=cosine[:, t], in_=cosine[:, t], func=ACT.Copy, scale=-2.0, bias=1.0
             )
-            sin_tab = const.tile(both, F32, name="sin_tab")
-            nc.vector.tensor_tensor(
-                out=sin_tab[:], in0=sine[:].unsqueeze(2).to_broadcast(both), in1=zoom[:],
-                op=ALU.mult,
+
+        def table_products(first_tile):
+            t = slice(first_tile, first_tile + ROUND)
+            shape = [P, ROUND, 2, PAIRS]
+            nc.gpsimd.tensor_tensor(
+                out=cos_tab[:, t], in0=cosine[:, t].unsqueeze(2).to_broadcast(shape),
+                in1=zoom[:, t], op=ALU.mult,
             )
-            return cos_tab, sin_tab
+            nc.gpsimd.tensor_tensor(
+                out=sin_tab[:, t], in0=sine[:, t].unsqueeze(2).to_broadcast(shape),
+                in1=zoom[:, t], op=ALU.mult,
+            )
 
         def rotate(qk, t, rotated):
             y = qk[:].rearrange("p (mj e) -> p mj e", e=2)
@@ -223,7 +240,7 @@ def tile_retblock_pa_kernel(tc, x, w_q, w_k, w_v, out_0, out_1, out_2):
                 op0=ALU.mult, op1=ALU.mult,
             )
             nc.vector.tensor_tensor(out=crossed[:, 1, :], in0=y[:, :, 0], in1=sin_t, op=ALU.mult)
-            nc.vector.tensor_tensor(
+            nc.gpsimd.tensor_tensor(
                 out=rotated.rearrange("p m (j e) -> p m j e", e=2),
                 in0=straight[:].rearrange("p (m j) e -> p m j e", m=2),
                 in1=crossed[:].rearrange("p e (m j) -> p m j e", m=2),
@@ -239,19 +256,30 @@ def tile_retblock_pa_kernel(tc, x, w_q, w_k, w_v, out_0, out_1, out_2):
         make_identity(nc, ident[:])
 
         x_raw = {}
+        wq_raw = load_w(w_q, "wq_raw")
         x_raw[0] = load_x(0)
-        w_raw = [load_w(w_q, "wq_raw"), load_w(w_k, "wk_raw"), load_w(w_v, "wv_raw")]
-        for r in range(1, AHEAD):
+        wk_raw = load_w(w_k, "wk_raw")
+        x_raw[1] = load_x(1)
+        wv_raw = load_w(w_v, "wv_raw")
+        for r in range(2, AHEAD):
             x_raw[r] = load_x(r)
 
-        cos_tab, sin_tab = build_tables()
+        log_base, centred, pos_turns, freq = table_columns()
+        table_zoom(log_base, centred)
+        table_turns(pos_turns, freq)
 
         x_mx = {}
         x_grouped = transpose_x(x_raw[0])
-        w_mx = [quantise_w(w_raw[0], "wq")]
+        wq_grouped = regroup_w(wq_raw)
+        table_fraction()
+        wq_mx = quantise_w(wq_grouped, "wq")
+        wk_grouped = regroup_w(wk_raw)
         x_mx[0] = quantise_x(x_grouped)
-        w_mx.append(quantise_w(w_raw[1], "wk"))
-        w_mx.append(quantise_w(w_raw[2], "wv"))
+        wk_mx = quantise_w(wk_grouped, "wk")
+        wv_grouped = regroup_w(wv_raw)
+        table_waves(0)
+        table_products(0)
+        wv_mx = quantise_w(wv_grouped, "wv")
 
         for r in range(ROUNDS):
             if r + 1 < ROUNDS:
@@ -260,20 +288,28 @@ def tile_retblock_pa_kernel(tc, x, w_q, w_k, w_v, out_0, out_1, out_2):
                 x_raw[r + AHEAD] = load_x(r + AHEAD)
 
             qk_banks = []
-            v_bank = v_psum.tile([P, ROUND, DH], F32, name="v_bank")
             for i in range(ROUND):
                 qk = qk_psum.tile([P, 2 * DH], F32, name="qk")
-                project(qk[:, 0:DH], x_mx[r], i, w_mx[0])
-                project(qk[:, DH : 2 * DH], x_mx[r], i, w_mx[1])
-                project(v_bank[:, i, :], x_mx[r], i, w_mx[2])
+                project(qk[:, 0:DH], x_mx[r], i, wq_mx)
+                project(qk[:, DH : 2 * DH], x_mx[r], i, wk_mx)
                 qk_banks.append(qk)
+            v_bank = v_psum.tile([P, ROUND, DH], F32, name="v_bank")
+            for i in range(ROUND):
+                project(v_bank[:, i, :], x_mx[r], i, wv_mx)
 
             if r + 1 < ROUNDS:
                 x_mx[r + 1] = quantise_x(x_grouped)
 
+            next_tiles = first_tile_of(r) + ROUND
+            make_tables = batch_of(r) == 0 and next_tiles < TILES
+            if make_tables:
+                table_waves(next_tiles)
+
             rotated = work.tile([P, 2, ROUND, DH], F32, name="rotated")
             for i in range(ROUND):
                 rotate(qk_banks[i], first_tile_of(r) + i, rotated[:, :, i, :])
+            if make_tables:
+                table_products(next_tiles)
             v_rows = work.tile([P, ROUND * DH], F32, name="v_rows")
             nc.scalar.copy(out=v_rows[:], in_=v_bank[:].rearrange("p i d -> p (i d)"))
 

@@ -240,7 +240,7 @@ def tile_retblock_pa_kernel(tc, x, w_q, w_k, w_v, out_0, out_1, out_2):
                 op0=ALU.mult, op1=ALU.mult,
             )
             nc.vector.tensor_tensor(out=crossed[:, 1, :], in0=y[:, :, 0], in1=sin_t, op=ALU.mult)
-            nc.gpsimd.tensor_tensor(
+            nc.vector.tensor_tensor(
                 out=rotated.rearrange("p m (j e) -> p m j e", e=2),
                 in0=straight[:].rearrange("p (m j) e -> p m j e", m=2),
                 in1=crossed[:].rearrange("p e (m j) -> p m j e", m=2),

@@ -179,7 +179,7 @@ def tile_retblock_pa_kernel(tc, x, w_q, w_k, w_v, out_0, out_1, out_2):
 
         def table_zoom(log_base, centred):
             log_z = const.tile(plain, F32, name="log_z")
-            nc.gpsimd.tensor_tensor(
+            nc.vector.tensor_tensor(
                 out=log_z[:],
                 in0=centred[:].unsqueeze(2).to_broadcast(plain),
                 in1=log_base[:].unsqueeze(1).to_broadcast(plain),
@@ -189,7 +189,7 @@ def tile_retblock_pa_kernel(tc, x, w_q, w_k, w_v, out_0, out_1, out_2):
             nc.scalar.activation(out=zoom[:, :, 1, :], in_=log_z[:], func=ACT.Exp, scale=-1.0)
 
         def table_turns(pos_turns, freq):
-            nc.gpsimd.tensor_tensor(
+            nc.vector.tensor_tensor(
                 out=angle[:],
                 in0=pos_turns[:].unsqueeze(2).to_broadcast(plain),
                 in1=freq[:].unsqueeze(1).to_broadcast(plain),
@@ -202,7 +202,7 @@ def tile_retblock_pa_kernel(tc, x, w_q, w_k, w_v, out_0, out_1, out_2):
                 out=whole[:], in0=angle[:], scalar1=ROUND_MAGIC, scalar2=ROUND_MAGIC,
                 op0=ALU.add, op1=ALU.subtract,
             )
-            nc.gpsimd.tensor_tensor(out=angle[:], in0=angle[:], in1=whole[:], op=ALU.subtract)
+            nc.vector.tensor_tensor(out=angle[:], in0=angle[:], in1=whole[:], op=ALU.subtract)
 
         def table_waves(first_tile):
             t = slice(first_tile, first_tile + ROUND)
@@ -216,11 +216,11 @@ def tile_retblock_pa_kernel(tc, x, w_q, w_k, w_v, out_0, out_1, out_2):
         def table_products(first_tile):
             t = slice(first_tile, first_tile + ROUND)
             shape = [P, ROUND, 2, PAIRS]
-            nc.gpsimd.tensor_tensor(
+            nc.vector.tensor_tensor(
                 out=cos_tab[:, t], in0=cosine[:, t].unsqueeze(2).to_broadcast(shape),
                 in1=zoom[:, t], op=ALU.mult,
             )
-            nc.gpsimd.tensor_tensor(
+            nc.vector.tensor_tensor(
                 out=sin_tab[:, t], in0=sine[:, t].unsqueeze(2).to_broadcast(shape),
                 in1=zoom[:, t], op=ALU.mult,
             )
@@ -240,7 +240,7 @@ def tile_retblock_pa_kernel(tc, x, w_q, w_k, w_v, out_0, out_1, out_2):
                 op0=ALU.mult, op1=ALU.mult,
             )
             nc.vector.tensor_tensor(out=crossed[:, 1, :], in0=y[:, :, 0], in1=sin_t, op=ALU.mult)
-            nc.vector.tensor_tensor(
+            nc.gpsimd.tensor_tensor(
                 out=rotated.rearrange("p m (j e) -> p m j e", e=2),
                 in0=straight[:].rearrange("p (m j) e -> p m j e", m=2),
                 in1=crossed[:].rearrange("p e (m j) -> p m j e", m=2),

@@ -23,6 +23,7 @@ WORDS = HID // 2
 ROUND = 2
 ROUNDS = BATCH * TILES // ROUND
 AHEAD = 5
+LAG = 1
 
 ROTARY_BASE = 10000.0
 SCALE_BASE = 512.0
@@ -36,7 +37,8 @@ def tile_retblock_pa_kernel(tc, x, w_q, w_k, w_v, out_0, out_1, out_2):
     with ExitStack() as ctx:
         const = ctx.enter_context(tc.tile_pool(name="const", bufs=1))
         x_raw_pool = ctx.enter_context(tc.tile_pool(name="x_raw_pool", bufs=AHEAD))
-        x_mx_pool = ctx.enter_context(tc.tile_pool(name="x_mx_pool", bufs=3))
+        x_grouped_pool = ctx.enter_context(tc.tile_pool(name="x_grouped_pool", bufs=3))
+        x_mx_pool = ctx.enter_context(tc.tile_pool(name="x_mx_pool", bufs=3 + LAG))
         w_grouped_pool = ctx.enter_context(tc.tile_pool(name="w_grouped_pool", bufs=2))
         work = ctx.enter_context(tc.tile_pool(name="work", bufs=3))
         xt_psum = ctx.enter_context(tc.psum_pool(name="xt_psum", bufs=4))
@@ -65,12 +67,12 @@ def tile_retblock_pa_kernel(tc, x, w_q, w_k, w_v, out_0, out_1, out_2):
             )
             return w_raw
 
-        def regroup_w(w_raw):
+        def regroup_w(copy, w_raw):
             w_grouped = w_grouped_pool.tile(
                 [P, PASSES, DH, PACK], BF16, align_bytes=64, name="w_grouped"
             )
             for g in range(PASSES):
-                nc.vector.tensor_copy(
+                copy(
                     out=w_grouped[:, g].rearrange("p (c i) t -> p c t i", i=4),
                     in_=w_raw[:, g * PACK : (g + 1) * PACK, :].rearrange(
                         "p t (c i) -> p c t i", i=4
@@ -90,7 +92,9 @@ def tile_retblock_pa_kernel(tc, x, w_q, w_k, w_v, out_0, out_1, out_2):
 
         def transpose_x(x_raw):
             words = x_raw[:].bitcast(F32)
-            x_grouped = x_mx_pool.tile([P, ROUND * HID], BF16, align_bytes=64, name="x_grouped")
+            x_grouped = x_grouped_pool.tile(
+                [P, ROUND * HID], BF16, align_bytes=64, name="x_grouped"
+            )
             grouped_words = x_grouped[:].bitcast(F32)
             for bank in range(ROUND * WORDS // (4 * P)):
                 xt = xt_psum.tile([P, 4, P], F32, name="xt")
@@ -137,6 +141,7 @@ def tile_retblock_pa_kernel(tc, x, w_q, w_k, w_v, out_0, out_1, out_2):
         plain = [P, TILES, PAIRS]
         both = [P, TILES, 2, PAIRS]
         angle = const.tile(plain, F32, name="angle")
+        whole = const.tile(plain, F32, name="whole")
         zoom = const.tile(both, F32, name="zoom")
         sine = const.tile(plain, F32, name="sine")
         cosine = const.tile(plain, F32, name="cosine")
@@ -188,21 +193,22 @@ def tile_retblock_pa_kernel(tc, x, w_q, w_k, w_v, out_0, out_1, out_2):
             nc.scalar.activation(out=zoom[:, :, 0, :], in_=log_z[:], func=ACT.Exp)
             nc.scalar.activation(out=zoom[:, :, 1, :], in_=log_z[:], func=ACT.Exp, scale=-1.0)
 
-        def table_turns(pos_turns, freq):
+        def table_angles(first_tile):
+            t = slice(first_tile, first_tile + ROUND)
+            shape = [P, ROUND, PAIRS]
             nc.vector.tensor_tensor(
-                out=angle[:],
-                in0=pos_turns[:].unsqueeze(2).to_broadcast(plain),
-                in1=freq[:].unsqueeze(1).to_broadcast(plain),
+                out=angle[:, t],
+                in0=pos_turns[:, t].unsqueeze(2).to_broadcast(shape),
+                in1=freq[:].unsqueeze(1).to_broadcast(shape),
                 op=ALU.mult,
             )
-
-        def table_fraction():
-            whole = const.tile(plain, F32, name="whole")
             nc.vector.tensor_scalar(
-                out=whole[:], in0=angle[:], scalar1=ROUND_MAGIC, scalar2=ROUND_MAGIC,
+                out=whole[:, t], in0=angle[:, t], scalar1=ROUND_MAGIC, scalar2=ROUND_MAGIC,
                 op0=ALU.add, op1=ALU.subtract,
             )
-            nc.vector.tensor_tensor(out=angle[:], in0=angle[:], in1=whole[:], op=ALU.subtract)
+            nc.vector.tensor_tensor(
+                out=angle[:, t], in0=angle[:, t], in1=whole[:, t], op=ALU.subtract
+            )
 
         def table_waves(first_tile):
             t = slice(first_tile, first_tile + ROUND)
@@ -252,67 +258,71 @@ def tile_retblock_pa_kernel(tc, x, w_q, w_k, w_v, out_0, out_1, out_2):
             first = first_tile_of(r) * DH
             nc.sync.dma_start(out=rows[:, first : first + ROUND * DH], in_=tile_rows)
 
-        ident = const.tile([P, P], F32, name="ident")
-        make_identity(nc, ident[:])
-
         x_raw = {}
         wq_raw = load_w(w_q, "wq_raw")
-        x_raw[0] = load_x(0)
         wk_raw = load_w(w_k, "wk_raw")
+        x_raw[0] = load_x(0)
         x_raw[1] = load_x(1)
         wv_raw = load_w(w_v, "wv_raw")
         for r in range(2, AHEAD):
             x_raw[r] = load_x(r)
 
         log_base, centred, pos_turns, freq = table_columns()
+        ident = const.tile([P, P], F32, name="ident")
+        make_identity(nc, ident[:])
         table_zoom(log_base, centred)
-        table_turns(pos_turns, freq)
+        table_angles(0)
+        table_waves(0)
 
         x_mx = {}
         x_grouped = transpose_x(x_raw[0])
-        wq_grouped = regroup_w(wq_raw)
-        table_fraction()
+        wq_grouped = regroup_w(nc.vector.tensor_copy, wq_raw)
+        wk_grouped = regroup_w(nc.vector.tensor_copy, wk_raw)
         wq_mx = quantise_w(wq_grouped, "wq")
-        wk_grouped = regroup_w(wk_raw)
-        x_mx[0] = quantise_x(x_grouped)
         wk_mx = quantise_w(wk_grouped, "wk")
-        wv_grouped = regroup_w(wv_raw)
-        table_waves(0)
+        x_mx[0] = quantise_x(x_grouped)
         table_products(0)
-        wv_mx = quantise_w(wv_grouped, "wv")
 
-        for r in range(ROUNDS):
+        for r in range(ROUNDS + LAG):
             if r + 1 < ROUNDS:
                 x_grouped = transpose_x(x_raw[r + 1])
             if r + AHEAD < ROUNDS:
                 x_raw[r + AHEAD] = load_x(r + AHEAD)
 
-            qk_banks = []
-            for i in range(ROUND):
-                qk = qk_psum.tile([P, 2 * DH], F32, name="qk")
-                project(qk[:, 0:DH], x_mx[r], i, wq_mx)
-                project(qk[:, DH : 2 * DH], x_mx[r], i, wk_mx)
-                qk_banks.append(qk)
-            v_bank = v_psum.tile([P, ROUND, DH], F32, name="v_bank")
-            for i in range(ROUND):
-                project(v_bank[:, i, :], x_mx[r], i, wv_mx)
+            if r < ROUNDS:
+                qk_banks = []
+                for i in range(ROUND):
+                    qk = qk_psum.tile([P, 2 * DH], F32, name="qk")
+                    project(qk[:, 0:DH], x_mx[r], i, wq_mx)
+                    project(qk[:, DH : 2 * DH], x_mx[r], i, wk_mx)
+                    qk_banks.append(qk)
+            if r >= LAG:
+                v_bank = v_psum.tile([P, ROUND, DH], F32, name="v_bank")
+                for i in range(ROUND):
+                    project(v_bank[:, i, :], x_mx[r - LAG], i, wv_mx)
 
             if r + 1 < ROUNDS:
                 x_mx[r + 1] = quantise_x(x_grouped)
 
+            if r < ROUNDS:
+                rotated = work.tile([P, 2, ROUND, DH], F32, name="rotated")
+                for i in range(ROUND):
+                    rotate(qk_banks[i], first_tile_of(r) + i, rotated[:, :, i, :])
+                store(out_0, r, rotated[:, 0].rearrange("p i d -> p (i d)"))
+                store(out_1, r, rotated[:, 1].rearrange("p i d -> p (i d)"))
+
+            if r == 0:
+                wv_grouped = regroup_w(nc.scalar.copy, wv_raw)
+                wv_mx = quantise_w(wv_grouped, "wv")
+
             next_tiles = first_tile_of(r) + ROUND
-            make_tables = batch_of(r) == 0 and next_tiles < TILES
-            if make_tables:
+            if next_tiles < TILES and batch_of(r) == 0:
+                table_angles(next_tiles)
+            if next_tiles < TILES and batch_of(r) == 1:
                 table_waves(next_tiles)
-
-            rotated = work.tile([P, 2, ROUND, DH], F32, name="rotated")
-            for i in range(ROUND):
-                rotate(qk_banks[i], first_tile_of(r) + i, rotated[:, :, i, :])
-            if make_tables:
                 table_products(next_tiles)
-            v_rows = work.tile([P, ROUND * DH], F32, name="v_rows")
-            nc.scalar.copy(out=v_rows[:], in_=v_bank[:].rearrange("p i d -> p (i d)"))
 
-            store(out_2, r, v_rows[:])
-            store(out_0, r, rotated[:, 0].rearrange("p i d -> p (i d)"))
-            store(out_1, r, rotated[:, 1].rearrange("p i d -> p (i d)"))
+            if r >= LAG:
+                v_rows = work.tile([P, ROUND * DH], F32, name="v_rows")
+                nc.scalar.copy(out=v_rows[:], in_=v_bank[:].rearrange("p i d -> p (i d)"))
+                store(out_2, r - LAG, v_rows[:])

@@ -23,7 +23,7 @@ WORDS = HID // 2
 ROUND = 2
 ROUNDS = BATCH * TILES // ROUND
 AHEAD = 5
-LAG = 1
+LAG = 2
 
 ROTARY_BASE = 10000.0
 SCALE_BASE = 512.0
@@ -41,6 +41,7 @@ def tile_retblock_pa_kernel(tc, x, w_q, w_k, w_v, out_0, out_1, out_2):
         x_mx_pool = ctx.enter_context(tc.tile_pool(name="x_mx_pool", bufs=3 + LAG))
         w_grouped_pool = ctx.enter_context(tc.tile_pool(name="w_grouped_pool", bufs=2))
         work = ctx.enter_context(tc.tile_pool(name="work", bufs=3))
+        terms = ctx.enter_context(tc.tile_pool(name="terms", bufs=4))
         xt_psum = ctx.enter_context(tc.psum_pool(name="xt_psum", bufs=4))
         qk_psum = ctx.enter_context(tc.psum_pool(name="qk_psum", bufs=3))
         v_psum = ctx.enter_context(tc.psum_pool(name="v_psum", bufs=1))
@@ -67,18 +68,20 @@ def tile_retblock_pa_kernel(tc, x, w_q, w_k, w_v, out_0, out_1, out_2):
             )
             return w_raw
 
-        def regroup_w(copy, w_raw):
+        def new_w_grouped():
             w_grouped = w_grouped_pool.tile(
                 [P, PASSES, DH, PACK], BF16, align_bytes=64, name="w_grouped"
             )
-            for g in range(PASSES):
+            return w_grouped
+
+        def regroup_w(copy, w_raw, w_grouped, passes):
+            for g in passes:
                 copy(
                     out=w_grouped[:, g].rearrange("p (c i) t -> p c t i", i=4),
                     in_=w_raw[:, g * PACK : (g + 1) * PACK, :].rearrange(
                         "p t (c i) -> p c t i", i=4
                     ),
                 )
-            return w_grouped
 
         def quantise_w(w_grouped, name):
             codes = const.tile([P, PASSES * DH], U32, align_bytes=64, name=name + "_codes")
@@ -110,17 +113,19 @@ def tile_retblock_pa_kernel(tc, x, w_q, w_k, w_v, out_0, out_1, out_2):
                 )
             return x_grouped
 
-        def quantise_x(x_grouped):
+        def new_x_mx():
             codes = x_mx_pool.tile([P, ROUND * PASSES * P], U32, align_bytes=64, name="x_codes")
             scales = x_mx_pool.tile([P, ROUND * PASSES * P], U8, align_bytes=64, name="x_scales")
-            for i in range(ROUND):
-                cols = slice(i * PASSES * P, (i + 1) * PASSES * P)
-                nc.vector.quantize_mx(
-                    out=codes[:, cols].bitcast(FP8X4),
-                    scales=scales[:, cols],
-                    in_=x_grouped[:, i * HID : (i + 1) * HID],
-                )
             return codes, scales
+
+        def quantise_x(x_grouped, x_mx, i):
+            codes, scales = x_mx
+            cols = slice(i * PASSES * P, (i + 1) * PASSES * P)
+            nc.vector.quantize_mx(
+                out=codes[:, cols].bitcast(FP8X4),
+                scales=scales[:, cols],
+                in_=x_grouped[:, i * HID : (i + 1) * HID],
+            )
 
         def project(out, x_mx, i, w_mx):
             x_codes, x_scales = x_mx
@@ -193,15 +198,14 @@ def tile_retblock_pa_kernel(tc, x, w_q, w_k, w_v, out_0, out_1, out_2):
             nc.scalar.activation(out=zoom[:, :, 0, :], in_=log_z[:], func=ACT.Exp)
             nc.scalar.activation(out=zoom[:, :, 1, :], in_=log_z[:], func=ACT.Exp, scale=-1.0)
 
-        def table_angles(first_tile):
-            t = slice(first_tile, first_tile + ROUND)
-            shape = [P, ROUND, PAIRS]
-            nc.vector.tensor_tensor(
-                out=angle[:, t],
-                in0=pos_turns[:, t].unsqueeze(2).to_broadcast(shape),
-                in1=freq[:].unsqueeze(1).to_broadcast(shape),
-                op=ALU.mult,
-            )
+        def table_angle():
+            for t in range(TILES):
+                nc.scalar.activation(
+                    out=angle[:, t, :], in_=freq[:], func=ACT.Copy, scale=pos_turns[:, t : t + 1]
+                )
+
+        def table_fraction(first_tile, end_tile):
+            t = slice(first_tile, end_tile)
             nc.vector.tensor_scalar(
                 out=whole[:, t], in0=angle[:, t], scalar1=ROUND_MAGIC, scalar2=ROUND_MAGIC,
                 op0=ALU.add, op1=ALU.subtract,
@@ -219,15 +223,10 @@ def tile_retblock_pa_kernel(tc, x, w_q, w_k, w_v, out_0, out_1, out_2):
                 out=cosine[:, t], in_=cosine[:, t], func=ACT.Copy, scale=-2.0, bias=1.0
             )
 
-        def table_products(first_tile):
+        def table_product(tab, wave, first_tile):
             t = slice(first_tile, first_tile + ROUND)
-            shape = [P, ROUND, 2, PAIRS]
             nc.vector.tensor_tensor(
-                out=cos_tab[:, t], in0=cosine[:, t].unsqueeze(2).to_broadcast(shape),
-                in1=zoom[:, t], op=ALU.mult,
-            )
-            nc.vector.tensor_tensor(
-                out=sin_tab[:, t], in0=sine[:, t].unsqueeze(2).to_broadcast(shape),
+                out=tab[:, t], in0=wave[:, t].unsqueeze(2).to_broadcast([P, ROUND, 2, PAIRS]),
                 in1=zoom[:, t], op=ALU.mult,
             )
 
@@ -235,12 +234,12 @@ def tile_retblock_pa_kernel(tc, x, w_q, w_k, w_v, out_0, out_1, out_2):
             y = qk[:].rearrange("p (mj e) -> p mj e", e=2)
             cos_t = cos_tab[:, t].rearrange("p m j -> p (m j)")
             sin_t = sin_tab[:, t].rearrange("p m j -> p (m j)")
-            straight = work.tile([P, 2 * PAIRS, 2], F32, name="straight")
+            straight = terms.tile([P, 2 * PAIRS, 2], F32, name="straight")
             nc.vector.tensor_tensor(
                 out=straight[:], in0=y, in1=cos_t.unsqueeze(2).to_broadcast([P, 2 * PAIRS, 2]),
                 op=ALU.mult,
             )
-            crossed = work.tile([P, 2, 2 * PAIRS], F32, name="crossed")
+            crossed = terms.tile([P, 2, 2 * PAIRS], F32, name="crossed")
             nc.vector.scalar_tensor_tensor(
                 out=crossed[:, 0, :], in0=y[:, :, 1], scalar=-1.0, in1=sin_t,
                 op0=ALU.mult, op1=ALU.mult,
@@ -270,22 +269,30 @@ def tile_retblock_pa_kernel(tc, x, w_q, w_k, w_v, out_0, out_1, out_2):
         log_base, centred, pos_turns, freq = table_columns()
         ident = const.tile([P, P], F32, name="ident")
         make_identity(nc, ident[:])
+        table_angle()
         table_zoom(log_base, centred)
-        table_angles(0)
+        table_fraction(0, ROUND)
         table_waves(0)
 
         x_mx = {}
         x_grouped = transpose_x(x_raw[0])
-        wq_grouped = regroup_w(nc.vector.tensor_copy, wq_raw)
-        wk_grouped = regroup_w(nc.vector.tensor_copy, wk_raw)
+        wq_grouped = new_w_grouped()
+        regroup_w(nc.vector.tensor_copy, wq_raw, wq_grouped, range(PASSES))
+        wk_grouped = new_w_grouped()
+        regroup_w(nc.vector.tensor_copy, wk_raw, wk_grouped, range(PASSES))
         wq_mx = quantise_w(wq_grouped, "wq")
         wk_mx = quantise_w(wk_grouped, "wk")
-        x_mx[0] = quantise_x(x_grouped)
-        table_products(0)
+        x_mx[0] = new_x_mx()
+        for i in range(ROUND):
+            quantise_x(x_grouped, x_mx[0], i)
+        tables = [(cos_tab, cosine), (sin_tab, sine)]
+        for tab, wave in tables:
+            table_product(tab, wave, 0)
 
         for r in range(ROUNDS + LAG):
             if r + 1 < ROUNDS:
                 x_grouped = transpose_x(x_raw[r + 1])
+                x_mx[r + 1] = new_x_mx()
             if r + AHEAD < ROUNDS:
                 x_raw[r + AHEAD] = load_x(r + AHEAD)
 
@@ -296,31 +303,39 @@ def tile_retblock_pa_kernel(tc, x, w_q, w_k, w_v, out_0, out_1, out_2):
                     project(qk[:, 0:DH], x_mx[r], i, wq_mx)
                     project(qk[:, DH : 2 * DH], x_mx[r], i, wk_mx)
                     qk_banks.append(qk)
+                rotated = work.tile([P, 2, ROUND, DH], F32, name="rotated")
             if r >= LAG:
                 v_bank = v_psum.tile([P, ROUND, DH], F32, name="v_bank")
                 for i in range(ROUND):
                     project(v_bank[:, i, :], x_mx[r - LAG], i, wv_mx)
 
-            if r + 1 < ROUNDS:
-                x_mx[r + 1] = quantise_x(x_grouped)
+            next_tiles = first_tile_of(r) + ROUND
+            make_tables = next_tiles < TILES and batch_of(r) == 1
+            if make_tables:
+                table_waves(next_tiles)
+
+            if r < LAG:
+                if r == 0:
+                    wv_grouped = new_w_grouped()
+                share = PASSES // LAG
+                regroup_w(nc.scalar.copy, wv_raw, wv_grouped, range(r * share, (r + 1) * share))
 
             if r < ROUNDS:
-                rotated = work.tile([P, 2, ROUND, DH], F32, name="rotated")
+                rotate(qk_banks[0], first_tile_of(r), rotated[:, :, 0, :])
+            if r + 1 < ROUNDS:
                 for i in range(ROUND):
-                    rotate(qk_banks[i], first_tile_of(r) + i, rotated[:, :, i, :])
+                    quantise_x(x_grouped, x_mx[r + 1], i)
+            if r == 0:
+                table_fraction(ROUND, TILES)
+            if make_tables:
+                for tab, wave in tables:
+                    table_product(tab, wave, next_tiles)
+            if r == LAG - 1:
+                wv_mx = quantise_w(wv_grouped, "wv")
+            if r < ROUNDS:
+                rotate(qk_banks[1], first_tile_of(r) + 1, rotated[:, :, 1, :])
                 store(out_0, r, rotated[:, 0].rearrange("p i d -> p (i d)"))
                 store(out_1, r, rotated[:, 1].rearrange("p i d -> p (i d)"))
-
-            if r == 0:
-                wv_grouped = regroup_w(nc.scalar.copy, wv_raw)
-                wv_mx = quantise_w(wv_grouped, "wv")
-
-            next_tiles = first_tile_of(r) + ROUND
-            if next_tiles < TILES and batch_of(r) == 0:
-                table_angles(next_tiles)
-            if next_tiles < TILES and batch_of(r) == 1:
-                table_waves(next_tiles)
-                table_products(next_tiles)
 
             if r >= LAG:
                 v_rows = work.tile([P, ROUND * DH], F32, name="v_rows")

from contextlib import ExitStack
import math

import concourse.mybir as mybir
from concourse.masks import make_identity

F32 = mybir.dt.float32
BF16 = mybir.dt.bfloat16
I32 = mybir.dt.int32
U32 = mybir.dt.uint32
U8 = mybir.dt.uint8
FP8X4 = mybir.dt.float8_e4m3fn_x4
ALU = mybir.AluOpType
ACT = mybir.ActivationFunctionType

P = 128
BATCH, SEQ, HID, DH = 2, 1024, 2048, 256
PAIRS = DH // 2
TILES = SEQ // P
PACK = 4
PASSES = HID // (P * PACK)
WORDS = HID // 2
ROUND = 2
ROUNDS = BATCH * TILES // ROUND
AHEAD = 5
LAG = 2

ROTARY_BASE = 10000.0
SCALE_BASE = 512.0
ROUND_MAGIC = 1.5 * 2.0**23

FLOPS = 2 * BATCH * SEQ * HID * 3 * DH


def tile_retblock_pa_kernel(tc, x, w_q, w_k, w_v, out_0, out_1, out_2):
    nc = tc.nc
    with ExitStack() as ctx:
        const = ctx.enter_context(tc.tile_pool(name="const", bufs=1))
        x_raw_pool = ctx.enter_context(tc.tile_pool(name="x_raw_pool", bufs=AHEAD))
        x_grouped_pool = ctx.enter_context(tc.tile_pool(name="x_grouped_pool", bufs=3))
        x_mx_pool = ctx.enter_context(tc.tile_pool(name="x_mx_pool", bufs=3 + LAG))
        w_grouped_pool = ctx.enter_context(tc.tile_pool(name="w_grouped_pool", bufs=2))
        work = ctx.enter_context(tc.tile_pool(name="work", bufs=3))
        terms = ctx.enter_context(tc.tile_pool(name="terms", bufs=4))
        xt_psum = ctx.enter_context(tc.psum_pool(name="xt_psum", bufs=4))
        qk_psum = ctx.enter_context(tc.psum_pool(name="qk_psum", bufs=3))
        v_psum = ctx.enter_context(tc.psum_pool(name="v_psum", bufs=1))
        ctx.enter_context(tc.manual_schedule())

        def batch_of(r):
            return r % BATCH

        def first_tile_of(r):
            return (r // BATCH) * ROUND

        def load_x(r):
            x_raw = x_raw_pool.tile([P, ROUND * HID], BF16, name="x_raw")
            rows = x[batch_of(r)].rearrange("(p t) k -> p (t k)", t=TILES)
            first = first_tile_of(r) * HID
            nc.sync.dma_start(out=x_raw[:], in_=rows[:, first : first + ROUND * HID])
            return x_raw

        def load_w(w, name):
            w_raw = const.tile([P, PASSES * PACK, DH], BF16, name=name)
            nc.sync.dma_start(
                out=w_raw[:].rearrange("p (a e) c -> p a (e c)", e=2),
                in_=w.rearrange("(a p e) c -> p a (e c)", p=P, e=2),
            )
            return w_raw

        def new_w_grouped():
            w_grouped = w_grouped_pool.tile(
                [P, PASSES, DH, PACK], BF16, align_bytes=64, name="w_grouped"
            )
            return w_grouped

        def regroup_w(copy, w_raw, w_grouped, passes):
            for g in passes:
                copy(
                    out=w_grouped[:, g].rearrange("p (c i) t -> p c t i", i=4),
                    in_=w_raw[:, g * PACK : (g + 1) * PACK, :].rearrange(
                        "p t (c i) -> p c t i", i=4
                    ),
                )

        def quantise_w(w_grouped, name):
            codes = const.tile([P, PASSES * DH], U32, align_bytes=64, name=name + "_codes")
            scales = const.tile([P, PASSES * DH], U8, align_bytes=64, name=name + "_scales")
            nc.vector.quantize_mx(
                out=codes[:].bitcast(FP8X4),
                scales=scales[:],
                in_=w_grouped[:].rearrange("p g c t -> p (g c t)"),
            )
            return codes, scales

        def transpose_x(x_raw):
            words = x_raw[:].bitcast(F32)
            x_grouped = x_grouped_pool.tile(
                [P, ROUND * HID], BF16, align_bytes=64, name="x_grouped"
            )
            grouped_words = x_grouped[:].bitcast(F32)
            for bank in range(ROUND * WORDS // (4 * P)):
                xt = xt_psum.tile([P, 4, P], F32, name="xt")
                for a in range(4):
                    first = (bank * 4 + a) * P
                    nc.tensor.transpose(xt[:, a, :], words[:, first : first + P], ident[:])
                first = bank * 4 * P
                nc.scalar.copy(
                    out=grouped_words[:, first : first + 4 * P].rearrange(
                        "p (g r u) -> p g r u", g=2, u=2
                    ),
                    in_=xt[:].rearrange("p (g u) r -> p g r u", u=2),
                )
            return x_grouped

        def new_x_mx():
            codes = x_mx_pool.tile([P, ROUND * PASSES * P], U32, align_bytes=64, name="x_codes")
            scales = x_mx_pool.tile([P, ROUND * PASSES * P], U8, align_bytes=64, name="x_scales")
            return codes, scales

        def quantise_x(x_grouped, x_mx, i):
            codes, scales = x_mx
            cols = slice(i * PASSES * P, (i + 1) * PASSES * P)
            nc.vector.quantize_mx(
                out=codes[:, cols].bitcast(FP8X4),
                scales=scales[:, cols],
                in_=x_grouped[:, i * HID : (i + 1) * HID],
            )

        def project(out, x_mx, i, w_mx):
            x_codes, x_scales = x_mx
            w_codes, w_scales = w_mx
            for g in range(PASSES):
                tokens = slice((i * PASSES + g) * P, (i * PASSES + g + 1) * P)
                features = slice(g * DH, (g + 1) * DH)
                nc.tensor.matmul_mx(
                    out=out,
                    lhsT=x_codes[:, tokens].bitcast(FP8X4),
                    lhsT_scale=x_scales[:, tokens],
                    rhs=w_codes[:, features].bitcast(FP8X4),
                    rhs_scale=w_scales[:, features],
                    start=(g == 0),
                    stop=(g == PASSES - 1),
                )

        plain = [P, TILES, PAIRS]
        both = [P, TILES, 2, PAIRS]
        angle = const.tile(plain, F32, name="angle")
        whole = const.tile(plain, F32, name="whole")
        zoom = const.tile(both, F32, name="zoom")
        sine = const.tile(plain, F32, name="sine")
        cosine = const.tile(plain, F32, name="cosine")
        cos_tab = const.tile(both, F32, name="cos_tab")
        sin_tab = const.tile(both, F32, name="sin_tab")

        def table_columns():
            j_int = const.tile([P, PAIRS], I32, name="j_int")
            nc.gpsimd.iota(j_int[:], pattern=[[1, PAIRS]], base=0, channel_multiplier=0)
            pos_int = const.tile([P, TILES], I32, name="pos_int")
            nc.gpsimd.iota(pos_int[:], pattern=[[1, TILES]], base=0, channel_multiplier=TILES)
            log_base = const.tile([P, PAIRS], F32, name="log_base")
            nc.vector.tensor_copy(out=log_base[:], in_=j_int[:])
            nc.vector.tensor_scalar(
                out=log_base[:], in0=log_base[:], scalar1=2.0 / (1.4 * DH), scalar2=0.4 / 1.4,
                op0=ALU.mult, op1=ALU.add,
            )
            nc.scalar.activation(out=log_base[:], in_=log_base[:], func=ACT.Ln)
            pos = const.tile([P, TILES], F32, name="pos")
            nc.vector.tensor_copy(out=pos[:], in_=pos_int[:])
            centred = const.tile([P, TILES], F32, name="centred")
            nc.vector.tensor_scalar(
                out=centred[:], in0=pos[:], scalar1=float(SEQ // 2), scalar2=1.0 / SCALE_BASE,
                op0=ALU.subtract, op1=ALU.mult,
            )
            pos_turns = const.tile([P, TILES], F32, name="pos_turns")
            nc.vector.tensor_scalar(
                out=pos_turns[:], in0=pos[:], scalar1=1.0 / (2.0 * math.pi), scalar2=None,
                op0=ALU.mult,
            )
            freq = const.tile([P, PAIRS], F32, name="freq")
            nc.vector.memset(freq[:, 0:1], 1.0)
            for doubling in range(7):
                width = 2**doubling
                nc.vector.tensor_scalar(
                    out=freq[:, width : 2 * width], in0=freq[:, 0:width],
                    scalar1=ROTARY_BASE ** (-width / PAIRS), scalar2=None, op0=ALU.mult,
                )
            return log_base, centred, pos_turns, freq

        def table_zoom(log_base, centred):
            log_z = const.tile(plain, F32, name="log_z")
            nc.vector.tensor_tensor(
                out=log_z[:],
                in0=centred[:].unsqueeze(2).to_broadcast(plain),
                in1=log_base[:].unsqueeze(1).to_broadcast(plain),
                op=ALU.mult,
            )
            nc.scalar.activation(out=zoom[:, :, 0, :], in_=log_z[:], func=ACT.Exp)
            nc.scalar.activation(out=zoom[:, :, 1, :], in_=log_z[:], func=ACT.Exp, scale=-1.0)

        def table_angle():
            for t in range(TILES):
                nc.scalar.activation(
                    out=angle[:, t, :], in_=freq[:], func=ACT.Copy, scale=pos_turns[:, t : t + 1]
                )

        def table_fraction(first_tile, end_tile):
            t = slice(first_tile, end_tile)
            nc.vector.tensor_scalar(
                out=whole[:, t], in0=angle[:, t], scalar1=ROUND_MAGIC, scalar2=ROUND_MAGIC,
                op0=ALU.add, op1=ALU.subtract,
            )
            nc.vector.tensor_tensor(
                out=angle[:, t], in0=angle[:, t], in1=whole[:, t], op=ALU.subtract
            )

        def table_waves(first_tile):
            t = slice(first_tile, first_tile + ROUND)
            nc.scalar.activation(out=cosine[:, t], in_=angle[:, t], func=ACT.Sin, scale=math.pi)
            nc.scalar.activation(out=sine[:, t], in_=angle[:, t], func=ACT.Sin, scale=2.0 * math.pi)
            nc.scalar.activation(out=cosine[:, t], in_=cosine[:, t], func=ACT.Square)
            nc.scalar.activation(
                out=cosine[:, t], in_=cosine[:, t], func=ACT.Copy, scale=-2.0, bias=1.0
            )

        def table_product(tab, wave, first_tile):
            t = slice(first_tile, first_tile + ROUND)
            nc.vector.tensor_tensor(
                out=tab[:, t], in0=wave[:, t].unsqueeze(2).to_broadcast([P, ROUND, 2, PAIRS]),
                in1=zoom[:, t], op=ALU.mult,
            )

        def rotate(qk, t, rotated):
            y = qk[:].rearrange("p (mj e) -> p mj e", e=2)
            cos_t = cos_tab[:, t].rearrange("p m j -> p (m j)")
            sin_t = sin_tab[:, t].rearrange("p m j -> p (m j)")
            straight = terms.tile([P, 2 * PAIRS, 2], F32, name="straight")
            nc.vector.tensor_tensor(
                out=straight[:], in0=y, in1=cos_t.unsqueeze(2).to_broadcast([P, 2 * PAIRS, 2]),
                op=ALU.mult,
            )
            crossed = terms.tile([P, 2, 2 * PAIRS], F32, name="crossed")
            nc.vector.scalar_tensor_tensor(
                out=crossed[:, 0, :], in0=y[:, :, 1], scalar=-1.0, in1=sin_t,
                op0=ALU.mult, op1=ALU.mult,
            )
            nc.vector.tensor_tensor(out=crossed[:, 1, :], in0=y[:, :, 0], in1=sin_t, op=ALU.mult)
            nc.gpsimd.tensor_tensor(
                out=rotated.rearrange("p m (j e) -> p m j e", e=2),
                in0=straight[:].rearrange("p (m j) e -> p m j e", m=2),
                in1=crossed[:].rearrange("p e (m j) -> p m j e", m=2),
                op=ALU.add,
            )

        def store(out, r, tile_rows):
            rows = out[batch_of(r)].rearrange("(p t) d -> p (t d)", t=TILES)
            first = first_tile_of(r) * DH
            nc.sync.dma_start(out=rows[:, first : first + ROUND * DH], in_=tile_rows)

        x_raw = {}
        wq_raw = load_w(w_q, "wq_raw")
        wk_raw = load_w(w_k, "wk_raw")
        x_raw[0] = load_x(0)
        x_raw[1] = load_x(1)
        wv_raw = load_w(w_v, "wv_raw")
        for r in range(2, AHEAD):
            x_raw[r] = load_x(r)

        log_base, centred, pos_turns, freq = table_columns()
        ident = const.tile([P, P], F32, name="ident")
        make_identity(nc, ident[:])
        table_angle()
        table_zoom(log_base, centred)
        table_fraction(0, ROUND)
        table_waves(0)

        x_mx = {}
        x_grouped = transpose_x(x_raw[0])
        wq_grouped = new_w_grouped()
        regroup_w(nc.vector.tensor_copy, wq_raw, wq_grouped, range(PASSES))
        wk_grouped = new_w_grouped()
        regroup_w(nc.vector.tensor_copy, wk_raw, wk_grouped, range(PASSES))
        wq_mx = quantise_w(wq_grouped, "wq")
        wk_mx = quantise_w(wk_grouped, "wk")
        x_mx[0] = new_x_mx()
        for i in range(ROUND):
            quantise_x(x_grouped, x_mx[0], i)
        tables = [(cos_tab, cosine), (sin_tab, sine)]
        for tab, wave in tables:
            table_product(tab, wave, 0)

        for r in range(ROUNDS + LAG):
            if r + 1 < ROUNDS:
                x_grouped = transpose_x(x_raw[r + 1])
                x_mx[r + 1] = new_x_mx()
            if r + AHEAD < ROUNDS:
                x_raw[r + AHEAD] = load_x(r + AHEAD)

            if r < ROUNDS:
                qk_banks = []
                for i in range(ROUND):
                    qk = qk_psum.tile([P, 2 * DH], F32, name="qk")
                    project(qk[:, 0:DH], x_mx[r], i, wq_mx)
                    project(qk[:, DH : 2 * DH], x_mx[r], i, wk_mx)
                    qk_banks.append(qk)
                rotated = work.tile([P, 2, ROUND, DH], F32, name="rotated")
            if r >= LAG:
                v_bank = v_psum.tile([P, ROUND, DH], F32, name="v_bank")
                for i in range(ROUND):
                    project(v_bank[:, i, :], x_mx[r - LAG], i, wv_mx)

            next_tiles = first_tile_of(r) + ROUND
            make_tables = next_tiles < TILES and batch_of(r) == 1
            if make_tables:
                table_waves(next_tiles)

            if r < LAG:
                if r == 0:
                    wv_grouped = new_w_grouped()
                share = PASSES // LAG
                regroup_w(nc.scalar.copy, wv_raw, wv_grouped, range(r * share, (r + 1) * share))

            if r < ROUNDS:
                rotate(qk_banks[0], first_tile_of(r), rotated[:, :, 0, :])
            if r + 1 < ROUNDS:
                for i in range(ROUND):
                    quantise_x(x_grouped, x_mx[r + 1], i)
            if r == 0:
                table_fraction(ROUND, TILES)
            if make_tables:
                for tab, wave in tables:
                    table_product(tab, wave, next_tiles)
            if r == LAG - 1:
                wv_mx = quantise_w(wv_grouped, "wv")
            if r < ROUNDS:
                rotate(qk_banks[1], first_tile_of(r) + 1, rotated[:, :, 1, :])
                store(out_0, r, rotated[:, 0].rearrange("p i d -> p (i d)"))
                store(out_1, r, rotated[:, 1].rearrange("p i d -> p (i d)"))

            if r >= LAG:
                v_rows = work.tile([P, ROUND * DH], F32, name="v_rows")
                nc.scalar.copy(out=v_rows[:], in_=v_bank[:].rearrange("p i d -> p (i d)"))
                store(out_2, r - LAG, v_rows[:])
